import numpy as np
import ml_dtypes


def mxq(x, axis, fmt="e4m3"):
    dtype, down = {"e4m3": (ml_dtypes.float8_e4m3fn, 7), "e5m2": (ml_dtypes.float8_e5m2, 14)}[fmt]
    v = np.moveaxis(np.asarray(x, np.float32).astype(ml_dtypes.bfloat16).astype(np.float64), axis, -1)
    blocks = v.reshape(v.shape[:-1] + (-1, 32))
    amax = np.abs(blocks).max(-1, keepdims=True)
    byte = np.maximum(np.where(amax > 0, np.frexp(amax)[1] - 1 + 127, 0) - down, 1)
    scale = np.exp2(byte - 127.0)
    codes = (blocks / scale).astype(np.float32).astype(dtype).astype(np.float64)
    return np.moveaxis((codes * scale).reshape(v.shape), -1, axis)


WIDE = False


def mx_kscale(k):
    if not WIDE:
        return np.ones(k)
    levels = np.array([10, -10, 5, -5, 0])
    a = np.random.permutation(np.resize(levels, k // 512 * 4)).reshape(k // 512, 4)
    idx = np.arange(k)
    return np.exp2(a[idx // 512, idx % 128 // 32])


BF16 = ml_dtypes.bfloat16


def bf(x):
    return np.asarray(x, np.float32).astype(BF16)


def f64(x):
    return np.asarray(x).astype(np.float64)


B, N, VD, QD, D, H, NG, P = 128, 36, 2048, 1024, 512, 2, 20, 64
DH = D // H


def setup_inputs():
    s = mx_kscale(D)
    return {"out_t": bf(np.random.standard_normal((B, N, H, D)) * 0.7 * s),
            "out_w": bf(np.random.standard_normal((H, D, DH)) / np.sqrt(D) / s[None, :, None]),
            "out_b": bf(np.random.standard_normal(D) * 0.3),
            "self_feat": bf(np.random.standard_normal((B, N, D)) * 0.9),
            "vis": bf(np.maximum(np.random.standard_normal((B, N, D)), 0.0))}


def reference(out_t, out_w, out_b, self_feat, vis):
    t = mxq(f64(out_t), 3, "e4m3").reshape(B * N, H, D).swapaxes(0, 1)
    nb = t @ mxq(f64(out_w), 1, "e4m3")
    neighbor = nb.swapaxes(0, 1).reshape(B, N, D) + f64(out_b)
    imp_rel = np.maximum(f64(self_feat) + neighbor, 0.0)
    return f64(vis) + imp_rel

@@ -1,0 +1,133 @@
+from contextlib import ExitStack
+
+import concourse.mybir as mybir
+from concourse.masks import make_identity
+
+F32 = mybir.dt.float32
+BF16 = mybir.dt.bfloat16
+U32 = mybir.dt.uint32
+U8 = mybir.dt.uint8
+FP8X4 = mybir.dt.float8_e4m3fn_x4
+ALU = mybir.AluOpType
+
+P = 128
+NOBJ = 36
+HEADS = 2
+K = 512
+DH = 256
+D = 512
+GT = 4
+GROUPS = NOBJ // GT
+
+FLOPS = 2 * P * NOBJ * HEADS * K * DH
+
+
+def tile_implicitrelationencoder_pb_t_kernel(tc, out_t, out_w, out_b, self_feat, vis, out):
+    nc = tc.nc
+    with ExitStack() as ctx:
+        const = ctx.enter_context(tc.tile_pool(name="const", bufs=1))
+        loads = ctx.enter_context(tc.tile_pool(name="loads", bufs=4))
+        work = ctx.enter_context(tc.tile_pool(name="work", bufs=2))
+        outs = ctx.enter_context(tc.tile_pool(name="outs", bufs=3))
+        psum_t = ctx.enter_context(tc.psum_pool(name="psum_t", bufs=4))
+        psum_a = ctx.enter_context(tc.psum_pool(name="psum_a", bufs=4))
+
+        ident = const.tile([P, P], F32)
+        make_identity(nc, ident[:])
+
+        x_tiles = []
+        s_tiles = []
+        v_tiles = []
+
+        def load_group(g):
+            n0 = g * GT
+            x = loads.tile([P, GT * HEADS * K], BF16, name="x%d" % g, tag="x")
+            nc.sync.dma_start(out=x[:], in_=out_t[:, n0 : n0 + GT].rearrange("b n h k -> b (n h k)"))
+            x_tiles.append(x)
+            if g == 0:
+                nc.sync.dma_start(
+                    out=wraw[:].rearrange("q h (u e) c -> q h u (e c)", u=2),
+                    in_=out_w.rearrange("h (u q e) c -> q h u (e c)", u=2, q=P, e=2),
+                )
+            s = loads.tile([P, GT * D], BF16, name="s%d" % g, tag="s")
+            nc.sync.dma_start(out=s[:], in_=self_feat[:, n0 : n0 + GT, :].rearrange("b n d -> b (n d)"))
+            s_tiles.append(s)
+            v = loads.tile([P, GT * D], BF16, name="v%d" % g, tag="v")
+            nc.sync.dma_start(out=v[:], in_=vis[:, n0 : n0 + GT, :].rearrange("b n d -> b (n d)"))
+            v_tiles.append(v)
+
+        wraw = const.tile([P, HEADS, 4, DH], BF16)
+        bias_bc = const.tile([P, D], BF16)
+        nc.scalar.dma_start(out=bias_bc[:], in_=out_b.partition_broadcast(P))
+
+        load_group(0)
+
+        wg = const.tile([P, HEADS, DH, 4], BF16, align_bytes=64)
+        nc.vector.tensor_copy(out=wg[:], in_=wraw[:].rearrange("q h t c -> q h c t"))
+        w_codes = const.tile([P, HEADS * DH], U32, align_bytes=64)
+        w_scales = const.tile([P, HEADS * DH], U8, align_bytes=64)
+        nc.vector.quantize_mx(
+            out=w_codes[:].bitcast(FP8X4),
+            scales=w_scales[:],
+            in_=wg[:].rearrange("q h c t -> q (h c t)"),
+        )
+
+        for g in range(GROUPS):
+            if g + 1 < GROUPS:
+                load_group(g + 1)
+            x = x_tiles[g]
+            s = s_tiles[g]
+            v = v_tiles[g]
+            xw = x[:].bitcast(F32)
+
+            grouped = work.tile([P, GT * HEADS * P * 4], BF16, align_bytes=64, tag="grouped")
+            gw = grouped[:].bitcast(F32)
+            codes = work.tile([P, GT * HEADS * P], U32, align_bytes=64, tag="codes")
+            scales = work.tile([P, GT * HEADS * P], U8, align_bytes=64, tag="scales")
+            for n in range(GT):
+                xt = psum_t.tile([P, HEADS, 2, P], F32, tag="xt")
+                for h in range(HEADS):
+                    for u in range(2):
+                        c0 = (n * HEADS + h) * 256 + u * P
+                        nc.tensor.transpose(xt[:, h, u, :], xw[:, c0 : c0 + P], ident[:])
+                nc.scalar.copy(
+                    out=gw[:, n * 512 : (n + 1) * 512].rearrange("q (h b u) -> q h b u", h=HEADS, u=2),
+                    in_=xt[:].rearrange("q h u b -> q h b u"),
+                )
+            for half in range(2):
+                nc.vector.quantize_mx(
+                    out=codes[:, half * 512 : (half + 1) * 512].bitcast(FP8X4),
+                    scales=scales[:, half * 512 : (half + 1) * 512],
+                    in_=grouped[:, half * 2048 : (half + 1) * 2048],
+                )
+
+            sfb = work.tile([P, GT, D], F32, tag="sfb")
+            nc.vector.tensor_tensor(
+                out=sfb[:],
+                in0=s[:].rearrange("p (n d) -> p n d", n=GT),
+                in1=bias_bc[:].unsqueeze(1).to_broadcast([P, GT, D]),
+                op=ALU.add,
+            )
+
+            o = outs.tile([P, GT * D], F32, tag="o")
+            for n in range(GT):
+                acc = psum_a.tile([P, D], F32, tag="acc")
+                for h in range(HEADS):
+                    m0 = (n * HEADS + h) * P
+                    nc.tensor.matmul_mx(
+                        out=acc[:, h * DH : (h + 1) * DH],
+                        lhsT=codes[:, m0 : m0 + P].bitcast(FP8X4),
+                        lhsT_scale=scales[:, m0 : m0 + P],
+                        rhs=w_codes[:, h * DH : (h + 1) * DH].bitcast(FP8X4),
+                        rhs_scale=w_scales[:, h * DH : (h + 1) * DH],
+                        start=True,
+                        stop=True,
+                    )
+                nc.vector.tensor_tensor(
+                    out=o[:, n * D : (n + 1) * D], in0=acc[:], in1=sfb[:, n, :], op=ALU.add
+                )
+            nc.vector.scalar_tensor_tensor(
+                out=o[:], in0=o[:], scalar=0.0, in1=v[:], op0=ALU.max, op1=ALU.add
+            )
+            n0 = g * GT
+            nc.gpsimd.dma_start(out=out[:, n0 : n0 + GT, :].rearrange("b n d -> b (n d)"), in_=o[:])

@@ -9,6 +9,7 @@ U32 = mybir.dt.uint32
 U8 = mybir.dt.uint8
 FP8X4 = mybir.dt.float8_e4m3fn_x4
 ALU = mybir.AluOpType
+ACT = mybir.ActivationFunctionType
 
 P = 128
 NOBJ = 36
@@ -18,49 +19,148 @@ DH = 256
 D = 512
 GT = 4
 GROUPS = NOBJ // GT
+NCOL = GT * P
 
 FLOPS = 2 * P * NOBJ * HEADS * K * DH
+UNITS = GROUPS * HEADS
 
 
 def tile_implicitrelationencoder_pb_t_kernel(tc, out_t, out_w, out_b, self_feat, vis, out):
     nc = tc.nc
     with ExitStack() as ctx:
         const = ctx.enter_context(tc.tile_pool(name="const", bufs=1))
-        loads = ctx.enter_context(tc.tile_pool(name="loads", bufs=4))
+        loads = ctx.enter_context(tc.tile_pool(name="loads", bufs=6))
         work = ctx.enter_context(tc.tile_pool(name="work", bufs=2))
+        upool = ctx.enter_context(tc.tile_pool(name="upool", bufs=4))
         outs = ctx.enter_context(tc.tile_pool(name="outs", bufs=3))
-        psum_t = ctx.enter_context(tc.psum_pool(name="psum_t", bufs=4))
-        psum_a = ctx.enter_context(tc.psum_pool(name="psum_a", bufs=4))
+        psum_t = ctx.enter_context(tc.psum_pool(name="psum_t", bufs=2))
+        psum_a = ctx.enter_context(tc.psum_pool(name="psum_a", bufs=2))
+        psum_b = ctx.enter_context(tc.psum_pool(name="psum_b", bufs=4))
+        ctx.enter_context(tc.manual_schedule())
 
         ident = const.tile([P, P], F32)
         make_identity(nc, ident[:])
 
-        x_tiles = []
-        s_tiles = []
-        v_tiles = []
+        x_tiles = {}
+        s_tiles = {}
+        v_tiles = {}
+        o_tiles = {}
+        grouped_tiles = {}
+        code_tiles = {}
+        u_tiles = {}
+        tb_tiles = {}
 
-        def load_group(g):
-            n0 = g * GT
+        def load_x(g, pieces):
             x = loads.tile([P, GT * HEADS * K], BF16, name="x%d" % g, tag="x")
-            nc.sync.dma_start(out=x[:], in_=out_t[:, n0 : n0 + GT].rearrange("b n h k -> b (n h k)"))
-            x_tiles.append(x)
-            if g == 0:
+            step = GT // pieces
+            for i in range(pieces):
+                n0 = g * GT + i * step
+                w = step * HEADS * K
                 nc.sync.dma_start(
-                    out=wraw[:].rearrange("q h (u e) c -> q h u (e c)", u=2),
-                    in_=out_w.rearrange("h (u q e) c -> q h u (e c)", u=2, q=P, e=2),
+                    out=x[:, i * w : (i + 1) * w],
+                    in_=out_t[:, n0 : n0 + step].rearrange("b n h k -> b (n h k)"),
                 )
-            s = loads.tile([P, GT * D], BF16, name="s%d" % g, tag="s")
-            nc.sync.dma_start(out=s[:], in_=self_feat[:, n0 : n0 + GT, :].rearrange("b n d -> b (n d)"))
-            s_tiles.append(s)
-            v = loads.tile([P, GT * D], BF16, name="v%d" % g, tag="v")
-            nc.sync.dma_start(out=v[:], in_=vis[:, n0 : n0 + GT, :].rearrange("b n d -> b (n d)"))
-            v_tiles.append(v)
+                if g == 0 and i == 0:
+                    nc.sync.dma_start(
+                        out=wraw[:].rearrange("q h (u e) c -> q h u (e c)", u=2),
+                        in_=out_w.rearrange("h (u q e) c -> q h u (e c)", u=2, q=P, e=2),
+                    )
+            x_tiles[g] = x
+
+        def load_sv(g):
+            n0 = g * GT
+            s = loads.tile([P, GT, D], BF16, name="s%d" % g, tag="s")
+            nc.sync.dma_start(out=s[:], in_=self_feat[:, n0 : n0 + GT, :])
+            s_tiles[g] = s
+            v = loads.tile([P, GT, D], BF16, name="v%d" % g, tag="v")
+            nc.sync.dma_start(out=v[:], in_=vis[:, n0 : n0 + GT, :])
+            v_tiles[g] = v
+
+        def transpose_in(unit):
+            g, h = divmod(unit, HEADS)
+            xw = x_tiles[g][:].bitcast(F32)
+            grouped = work.tile([P, NCOL * 4], BF16, align_bytes=64, name="grouped", tag="grouped")
+            gw = grouped[:].bitcast(F32)
+            for pair in range(2):
+                xt = psum_t.tile([P, 2, 2, P], F32, name="xt", tag="xt")
+                for n2 in range(2):
+                    for u in range(2):
+                        c0 = ((pair * 2 + n2) * HEADS + h) * 256 + u * P
+                        nc.tensor.transpose(xt[:, n2, u, :], xw[:, c0 : c0 + P], ident[:])
+                nc.scalar.copy(
+                    out=gw[:, pair * 512 : (pair + 1) * 512].rearrange("q (n b u) -> q n b u", n=2, u=2),
+                    in_=xt[:].rearrange("q n u b -> q n b u"),
+                )
+            grouped_tiles[unit] = grouped
+
+        def quantise(unit):
+            codes = work.tile([P, NCOL], U32, align_bytes=64, name="codes", tag="codes")
+            scales = work.tile([P, NCOL], U8, align_bytes=64, name="scales", tag="scales")
+            nc.vector.quantize_mx(out=codes[:].bitcast(FP8X4), scales=scales[:], in_=grouped_tiles[unit][:])
+            code_tiles[unit] = (codes, scales)
+
+        def multiply(unit):
+            h = unit % HEADS
+            codes, scales = code_tiles[unit]
+            us = []
+            for j in range(2):
+                cb = h * 2 + j
+                acc = psum_a.tile([P, NCOL], F32, name="acc", tag="acc")
+                nc.tensor.matmul_mx(
+                    out=acc[:],
+                    lhsT=w_codes[:, cb * P : (cb + 1) * P].bitcast(FP8X4),
+                    lhsT_scale=w_scales[:, cb * P : (cb + 1) * P],
+                    rhs=codes[:].bitcast(FP8X4),
+                    rhs_scale=scales[:],
+                    start=True,
+                    stop=True,
+                )
+                u_sb = upool.tile([P, NCOL], F32, name="u_sb", tag="u")
+                nc.scalar.activation(
+                    out=u_sb[:], in_=acc[:], func=ACT.Identity, bias=bias_col[:, cb : cb + 1], scale=1.0
+                )
+                us.append(u_sb)
+            u_tiles[unit] = us
+
+        def transpose_back(unit):
+            us = u_tiles[unit]
+            tbs = []
+            for pair in range(2):
+                tb = psum_b.tile([P, 2, DH], F32, name="tb", tag="tb")
+                for n2 in range(2):
+                    for j in range(2):
+                        r0 = (pair * 2 + n2) * P
+                        nc.tensor.transpose(tb[:, n2, j * P : (j + 1) * P], us[j][:, r0 : r0 + P], ident[:])
+                tbs.append(tb)
+            tb_tiles[unit] = tbs
+
+        def finish(unit):
+            g, h = divmod(unit, HEADS)
+            if h == 0:
+                o_tiles[g] = outs.tile([P, GT, D], F32, name="o", tag="o")
+            o = o_tiles[g]
+            cols = slice(h * DH, (h + 1) * DH)
+            for pair in range(2):
+                rows = slice(pair * 2, pair * 2 + 2)
+                nc.vector.tensor_tensor(
+                    out=o[:, rows, cols], in0=tb_tiles[unit][pair][:], in1=s_tiles[g][:, rows, cols], op=ALU.add
+                )
+            nc.vector.scalar_tensor_tensor(
+                out=o[:, :, cols], in0=o[:, :, cols], scalar=0.0, in1=v_tiles[g][:, :, cols], op0=ALU.max, op1=ALU.add
+            )
+            if h == HEADS - 1:
+                nc.sync.dma_start(out=out[:, g * GT : (g + 1) * GT, :], in_=o[:])
 
         wraw = const.tile([P, HEADS, 4, DH], BF16)
-        bias_bc = const.tile([P, D], BF16)
-        nc.scalar.dma_start(out=bias_bc[:], in_=out_b.partition_broadcast(P))
-
-        load_group(0)
+        bz = const.tile([P, P], BF16)
+        nc.vector.memset(bz[:], 0.0)
+        load_x(0, 2)
+        nc.sync.dma_start(out=bz[0:4, :], in_=out_b.rearrange("(j m) -> j m", j=4))
+        load_x(1, 1)
+        load_sv(0)
+        for g in range(2, 4):
+            load_x(g, 1)
+            load_sv(g - 1)
 
         wg = const.tile([P, HEADS, DH, 4], BF16, align_bytes=64)
         nc.vector.tensor_copy(out=wg[:], in_=wraw[:].rearrange("q h t c -> q h c t"))
@@ -71,63 +171,27 @@ def tile_implicitrelationencoder_pb_t_kernel(tc, out_t, out_w, out_b, self_feat,
             scales=w_scales[:],
             in_=wg[:].rearrange("q h c t -> q (h c t)"),
         )
+        bzf = const.tile([P, P], F32)
+        bias_col = const.tile([P, 4], F32)
 
-        for g in range(GROUPS):
-            if g + 1 < GROUPS:
-                load_group(g + 1)
-            x = x_tiles[g]
-            s = s_tiles[g]
-            v = v_tiles[g]
-            xw = x[:].bitcast(F32)
-
-            grouped = work.tile([P, GT * HEADS * P * 4], BF16, align_bytes=64, tag="grouped")
-            gw = grouped[:].bitcast(F32)
-            codes = work.tile([P, GT * HEADS * P], U32, align_bytes=64, tag="codes")
-            scales = work.tile([P, GT * HEADS * P], U8, align_bytes=64, tag="scales")
-            for n in range(GT):
-                xt = psum_t.tile([P, HEADS, 2, P], F32, tag="xt")
-                for h in range(HEADS):
-                    for u in range(2):
-                        c0 = (n * HEADS + h) * 256 + u * P
-                        nc.tensor.transpose(xt[:, h, u, :], xw[:, c0 : c0 + P], ident[:])
-                nc.scalar.copy(
-                    out=gw[:, n * 512 : (n + 1) * 512].rearrange("q (h b u) -> q h b u", h=HEADS, u=2),
-                    in_=xt[:].rearrange("q h u b -> q h b u"),
-                )
-            for half in range(2):
-                nc.vector.quantize_mx(
-                    out=codes[:, half * 512 : (half + 1) * 512].bitcast(FP8X4),
-                    scales=scales[:, half * 512 : (half + 1) * 512],
-                    in_=grouped[:, half * 2048 : (half + 1) * 2048],
-                )
-
-            sfb = work.tile([P, GT, D], F32, tag="sfb")
-            nc.vector.tensor_tensor(
-                out=sfb[:],
-                in0=s[:].rearrange("p (n d) -> p n d", n=GT),
-                in1=bias_bc[:].unsqueeze(1).to_broadcast([P, GT, D]),
-                op=ALU.add,
-            )
-
-            o = outs.tile([P, GT * D], F32, tag="o")
-            for n in range(GT):
-                acc = psum_a.tile([P, D], F32, tag="acc")
-                for h in range(HEADS):
-                    m0 = (n * HEADS + h) * P
-                    nc.tensor.matmul_mx(
-                        out=acc[:, h * DH : (h + 1) * DH],
-                        lhsT=codes[:, m0 : m0 + P].bitcast(FP8X4),
-                        lhsT_scale=scales[:, m0 : m0 + P],
-                        rhs=w_codes[:, h * DH : (h + 1) * DH].bitcast(FP8X4),
-                        rhs_scale=w_scales[:, h * DH : (h + 1) * DH],
-                        start=True,
-                        stop=True,
-                    )
-                nc.vector.tensor_tensor(
-                    out=o[:, n * D : (n + 1) * D], in0=acc[:], in1=sfb[:, n, :], op=ALU.add
-                )
-            nc.vector.scalar_tensor_tensor(
-                out=o[:], in0=o[:], scalar=0.0, in1=v[:], op0=ALU.max, op1=ALU.add
-            )
-            n0 = g * GT
-            nc.gpsimd.dma_start(out=out[:, n0 : n0 + GT, :].rearrange("b n d -> b (n d)"), in_=o[:])
+        for step in range(UNITS + 3):
+            if step % HEADS == 0:
+                g = step // HEADS + 4
+                if g < GROUPS:
+                    load_x(g, 1)
+                if g - 1 < GROUPS:
+                    load_sv(g - 1)
+            if step < UNITS:
+                transpose_in(step)
+            if step == 1:
+                nc.vector.tensor_copy(out=bzf[:], in_=bz[:])
+                bt = psum_b.tile([P, P], F32, name="bt", tag="tb")
+                nc.tensor.transpose(bt[:], bzf[:], ident[:])
+                nc.vector.tensor_copy(out=bias_col[:], in_=bt[:, 0:4])
+            if 0 <= step - 1 < UNITS:
+                quantise(step - 1)
+                multiply(step - 1)
+            if 0 <= step - 2 < UNITS:
+                transpose_back(step - 2)
+            if 0 <= step - 3 < UNITS:
+                finish(step - 3)

@@ -23,6 +23,7 @@ NCOL = GT * P
 
 FLOPS = 2 * P * NOBJ * HEADS * K * DH
 UNITS = GROUPS * HEADS
+FIRST_PE_ADD = 4
 
 
 def tile_implicitrelationencoder_pb_t_kernel(tc, out_t, out_w, out_b, self_feat, vis, out):
@@ -30,7 +31,8 @@ def tile_implicitrelationencoder_pb_t_kernel(tc, out_t, out_w, out_b, self_feat,
     with ExitStack() as ctx:
         const = ctx.enter_context(tc.tile_pool(name="const", bufs=1))
         loads = ctx.enter_context(tc.tile_pool(name="loads", bufs=6))
-        work = ctx.enter_context(tc.tile_pool(name="work", bufs=2))
+        gpool = ctx.enter_context(tc.tile_pool(name="gpool", bufs=2))
+        cpool = ctx.enter_context(tc.tile_pool(name="cpool", bufs=2))
         upool = ctx.enter_context(tc.tile_pool(name="upool", bufs=4))
         outs = ctx.enter_context(tc.tile_pool(name="outs", bufs=3))
         psum_t = ctx.enter_context(tc.psum_pool(name="psum_t", bufs=2))
@@ -40,6 +42,8 @@ def tile_implicitrelationencoder_pb_t_kernel(tc, out_t, out_w, out_b, self_feat,
 
         ident = const.tile([P, P], F32)
         make_identity(nc, ident[:])
+        ident_bf = const.tile([P, P], BF16)
+        make_identity(nc, ident_bf[:])
 
         x_tiles = {}
         s_tiles = {}
@@ -79,7 +83,7 @@ def tile_implicitrelationencoder_pb_t_kernel(tc, out_t, out_w, out_b, self_feat,
         def transpose_in(unit):
             g, h = divmod(unit, HEADS)
             xw = x_tiles[g][:].bitcast(F32)
-            grouped = work.tile([P, NCOL * 4], BF16, align_bytes=64, name="grouped", tag="grouped")
+            grouped = gpool.tile([P, NCOL * 4], BF16, align_bytes=64, name="grouped", tag="grouped")
             gw = grouped[:].bitcast(F32)
             for pair in range(2):
                 xt = psum_t.tile([P, 2, 2, P], F32, name="xt", tag="xt")
@@ -94,8 +98,8 @@ def tile_implicitrelationencoder_pb_t_kernel(tc, out_t, out_w, out_b, self_feat,
             grouped_tiles[unit] = grouped
 
         def quantise(unit):
-            codes = work.tile([P, NCOL], U32, align_bytes=64, name="codes", tag="codes")
-            scales = work.tile([P, NCOL], U8, align_bytes=64, name="scales", tag="scales")
+            codes = cpool.tile([P, NCOL], U32, align_bytes=64, name="codes", tag="codes")
+            scales = cpool.tile([P, NCOL], U8, align_bytes=64, name="scales", tag="scales")
             nc.vector.quantize_mx(out=codes[:].bitcast(FP8X4), scales=scales[:], in_=grouped_tiles[unit][:])
             code_tiles[unit] = (codes, scales)
 
@@ -123,14 +127,34 @@ def tile_implicitrelationencoder_pb_t_kernel(tc, out_t, out_w, out_b, self_feat,
             u_tiles[unit] = us
 
         def transpose_back(unit):
+            g, h = divmod(unit, HEADS)
             us = u_tiles[unit]
             tbs = []
             for pair in range(2):
                 tb = psum_b.tile([P, 2, DH], F32, name="tb", tag="tb")
+                pe_add = pair == 0 and unit >= FIRST_PE_ADD
                 for n2 in range(2):
+                    n = pair * 2 + n2
+                    if pe_add:
+                        nc.tensor.matmul(
+                            out=tb[:, n2, :],
+                            lhsT=ident_bf[:],
+                            rhs=s_tiles[g][:, n, h * DH : (h + 1) * DH],
+                            start=True,
+                            stop=False,
+                        )
                     for j in range(2):
-                        r0 = (pair * 2 + n2) * P
-                        nc.tensor.transpose(tb[:, n2, j * P : (j + 1) * P], us[j][:, r0 : r0 + P], ident[:])
+                        if pe_add:
+                            nc.tensor.matmul(
+                                out=tb[:, n2, j * P : (j + 1) * P],
+                                lhsT=us[j][:, n * P : (n + 1) * P],
+                                rhs=ident[:],
+                                is_transpose=True,
+                                start=False,
+                                stop=(j == 1),
+                            )
+                        else:
+                            nc.tensor.transpose(tb[:, n2, j * P : (j + 1) * P], us[j][:, n * P : (n + 1) * P], ident[:])
                 tbs.append(tb)
             tb_tiles[unit] = tbs
 
@@ -139,17 +163,35 @@ def tile_implicitrelationencoder_pb_t_kernel(tc, out_t, out_w, out_b, self_feat,
             if h == 0:
                 o_tiles[g] = outs.tile([P, GT, D], F32, name="o", tag="o")
             o = o_tiles[g]
+            v = v_tiles[g]
             cols = slice(h * DH, (h + 1) * DH)
-            for pair in range(2):
+            first_plain = 0
+            if unit >= FIRST_PE_ADD:
+                first_plain = 1
+                nc.vector.scalar_tensor_tensor(
+                    out=o[:, 0:2, cols], in0=tb_tiles[unit][0][:], scalar=0.0, in1=v[:, 0:2, cols],
+                    op0=ALU.max, op1=ALU.add,
+                )
+            for pair in range(first_plain, 2):
                 rows = slice(pair * 2, pair * 2 + 2)
                 nc.vector.tensor_tensor(
                     out=o[:, rows, cols], in0=tb_tiles[unit][pair][:], in1=s_tiles[g][:, rows, cols], op=ALU.add
                 )
+            rest = slice(first_plain * 2, GT)
             nc.vector.scalar_tensor_tensor(
-                out=o[:, :, cols], in0=o[:, :, cols], scalar=0.0, in1=v_tiles[g][:, :, cols], op0=ALU.max, op1=ALU.add
+                out=o[:, rest, cols], in0=o[:, rest, cols], scalar=0.0, in1=v[:, rest, cols],
+                op0=ALU.max, op1=ALU.add,
             )
-            if h == HEADS - 1:
-                nc.sync.dma_start(out=out[:, g * GT : (g + 1) * GT, :], in_=o[:])
+
+        def store(unit):
+            g, h = divmod(unit, HEADS)
+            o = o_tiles[g]
+            if g < GROUPS - 1:
+                if h == HEADS - 1:
+                    nc.sync.dma_start(out=out[:, g * GT : (g + 1) * GT, :], in_=o[:])
+            else:
+                cols = slice(h * DH, (h + 1) * DH)
+                nc.sync.dma_start(out=out[:, g * GT : (g + 1) * GT, cols], in_=o[:, :, cols])
 
         wraw = const.tile([P, HEADS, 4, DH], BF16)
         bz = const.tile([P, P], BF16)
@@ -161,6 +203,7 @@ def tile_implicitrelationencoder_pb_t_kernel(tc, out_t, out_w, out_b, self_feat,
         for g in range(2, 4):
             load_x(g, 1)
             load_sv(g - 1)
+
 
         wg = const.tile([P, HEADS, DH, 4], BF16, align_bytes=64)
         nc.vector.tensor_copy(out=wg[:], in_=wraw[:].rearrange("q h t c -> q h c t"))
@@ -181,17 +224,20 @@ def tile_implicitrelationencoder_pb_t_kernel(tc, out_t, out_w, out_b, self_feat,
                     load_x(g, 1)
                 if g - 1 < GROUPS:
                     load_sv(g - 1)
-            if step < UNITS:
+            if 0 <= step < UNITS:
                 transpose_in(step)
+            if 0 <= step - 1 < UNITS:
+                quantise(step - 1)
             if step == 1:
                 nc.vector.tensor_copy(out=bzf[:], in_=bz[:])
                 bt = psum_b.tile([P, P], F32, name="bt", tag="tb")
                 nc.tensor.transpose(bt[:], bzf[:], ident[:])
                 nc.vector.tensor_copy(out=bias_col[:], in_=bt[:, 0:4])
             if 0 <= step - 1 < UNITS:
-                quantise(step - 1)
                 multiply(step - 1)
             if 0 <= step - 2 < UNITS:
                 transpose_back(step - 2)
             if 0 <= step - 3 < UNITS:
                 finish(step - 3)
+            if 0 <= step - 3 < UNITS:
+                store(step - 3)

@@ -23,7 +23,11 @@ NCOL = GT * P
 
 FLOPS = 2 * P * NOBJ * HEADS * K * DH
 UNITS = GROUPS * HEADS
-FIRST_PE_ADD = 4
+FIRST_PE_ADD = 5
+
+
+def pe_adds(unit, pair):
+    return (pair == 0 and unit >= FIRST_PE_ADD) or unit == UNITS - 1
 
 
 def tile_implicitrelationencoder_pb_t_kernel(tc, out_t, out_w, out_b, self_feat, vis, out):
@@ -34,7 +38,7 @@ def tile_implicitrelationencoder_pb_t_kernel(tc, out_t, out_w, out_b, self_feat,
         gpool = ctx.enter_context(tc.tile_pool(name="gpool", bufs=2))
         cpool = ctx.enter_context(tc.tile_pool(name="cpool", bufs=2))
         upool = ctx.enter_context(tc.tile_pool(name="upool", bufs=4))
-        outs = ctx.enter_context(tc.tile_pool(name="outs", bufs=3))
+        outs = ctx.enter_context(tc.tile_pool(name="outs", bufs=5))
         psum_t = ctx.enter_context(tc.psum_pool(name="psum_t", bufs=2))
         psum_a = ctx.enter_context(tc.psum_pool(name="psum_a", bufs=2))
         psum_b = ctx.enter_context(tc.psum_pool(name="psum_b", bufs=4))
@@ -54,21 +58,9 @@ def tile_implicitrelationencoder_pb_t_kernel(tc, out_t, out_w, out_b, self_feat,
         u_tiles = {}
         tb_tiles = {}
 
-        def load_x(g, pieces):
-            x = loads.tile([P, GT * HEADS * K], BF16, name="x%d" % g, tag="x")
-            step = GT // pieces
-            for i in range(pieces):
-                n0 = g * GT + i * step
-                w = step * HEADS * K
-                nc.sync.dma_start(
-                    out=x[:, i * w : (i + 1) * w],
-                    in_=out_t[:, n0 : n0 + step].rearrange("b n h k -> b (n h k)"),
-                )
-                if g == 0 and i == 0:
-                    nc.sync.dma_start(
-                        out=wraw[:].rearrange("q h (u e) c -> q h u (e c)", u=2),
-                        in_=out_w.rearrange("h (u q e) c -> q h u (e c)", u=2, q=P, e=2),
-                    )
+        def load_x(g):
+            x = loads.tile([P, GT, HEADS, K], BF16, name="x%d" % g, tag="x")
+            nc.sync.dma_start(out=x[:], in_=out_t[:, g * GT : (g + 1) * GT])
             x_tiles[g] = x
 
         def load_sv(g):
@@ -82,7 +74,7 @@ def tile_implicitrelationencoder_pb_t_kernel(tc, out_t, out_w, out_b, self_feat,
 
         def transpose_in(unit):
             g, h = divmod(unit, HEADS)
-            xw = x_tiles[g][:].bitcast(F32)
+            xw = x_tiles[g][:].rearrange("p n h k -> p (n h k)").bitcast(F32)
             grouped = gpool.tile([P, NCOL * 4], BF16, align_bytes=64, name="grouped", tag="grouped")
             gw = grouped[:].bitcast(F32)
             for pair in range(2):
@@ -132,10 +124,9 @@ def tile_implicitrelationencoder_pb_t_kernel(tc, out_t, out_w, out_b, self_feat,
             tbs = []
             for pair in range(2):
                 tb = psum_b.tile([P, 2, DH], F32, name="tb", tag="tb")
-                pe_add = pair == 0 and unit >= FIRST_PE_ADD
                 for n2 in range(2):
                     n = pair * 2 + n2
-                    if pe_add:
+                    if pe_adds(unit, pair):
                         nc.tensor.matmul(
                             out=tb[:, n2, :],
                             lhsT=ident_bf[:],
@@ -143,8 +134,7 @@ def tile_implicitrelationencoder_pb_t_kernel(tc, out_t, out_w, out_b, self_feat,
                             start=True,
                             stop=False,
                         )
-                    for j in range(2):
-                        if pe_add:
+                        for j in range(2):
                             nc.tensor.matmul(
                                 out=tb[:, n2, j * P : (j + 1) * P],
                                 lhsT=us[j][:, n * P : (n + 1) * P],
@@ -153,7 +143,8 @@ def tile_implicitrelationencoder_pb_t_kernel(tc, out_t, out_w, out_b, self_feat,
                                 start=False,
                                 stop=(j == 1),
                             )
-                        else:
+                    else:
+                        for j in range(2):
                             nc.tensor.transpose(tb[:, n2, j * P : (j + 1) * P], us[j][:, n * P : (n + 1) * P], ident[:])
                 tbs.append(tb)
             tb_tiles[unit] = tbs
@@ -165,55 +156,61 @@ def tile_implicitrelationencoder_pb_t_kernel(tc, out_t, out_w, out_b, self_feat,
             o = o_tiles[g]
             v = v_tiles[g]
             cols = slice(h * DH, (h + 1) * DH)
-            first_plain = 0
-            if unit >= FIRST_PE_ADD:
-                first_plain = 1
+            n0 = g * GT
+            plain = [pair for pair in range(2) if not pe_adds(unit, pair)]
+            for pair in range(2):
+                rows = slice(pair * 2, pair * 2 + 2)
+                if pe_adds(unit, pair):
+                    nc.vector.scalar_tensor_tensor(
+                        out=o[:, rows, cols], in0=tb_tiles[unit][pair][:], scalar=0.0, in1=v[:, rows, cols],
+                        op0=ALU.max, op1=ALU.add,
+                    )
+                    if unit == UNITS - 1:
+                        nc.sync.dma_start(out=out[:, n0 + pair * 2 : n0 + pair * 2 + 2, cols], in_=o[:, rows, cols])
+                else:
+                    nc.vector.tensor_tensor(
+                        out=o[:, rows, cols], in0=tb_tiles[unit][pair][:], in1=s_tiles[g][:, rows, cols], op=ALU.add
+                    )
+            if plain:
+                rest = slice(plain[0] * 2, GT)
                 nc.vector.scalar_tensor_tensor(
-                    out=o[:, 0:2, cols], in0=tb_tiles[unit][0][:], scalar=0.0, in1=v[:, 0:2, cols],
+                    out=o[:, rest, cols], in0=o[:, rest, cols], scalar=0.0, in1=v[:, rest, cols],
                     op0=ALU.max, op1=ALU.add,
                 )
-            for pair in range(first_plain, 2):
-                rows = slice(pair * 2, pair * 2 + 2)
-                nc.vector.tensor_tensor(
-                    out=o[:, rows, cols], in0=tb_tiles[unit][pair][:], in1=s_tiles[g][:, rows, cols], op=ALU.add
-                )
-            rest = slice(first_plain * 2, GT)
-            nc.vector.scalar_tensor_tensor(
-                out=o[:, rest, cols], in0=o[:, rest, cols], scalar=0.0, in1=v[:, rest, cols],
-                op0=ALU.max, op1=ALU.add,
-            )
-
-        def store(unit):
-            g, h = divmod(unit, HEADS)
-            o = o_tiles[g]
             if g < GROUPS - 1:
                 if h == HEADS - 1:
-                    nc.sync.dma_start(out=out[:, g * GT : (g + 1) * GT, :], in_=o[:])
-            else:
-                cols = slice(h * DH, (h + 1) * DH)
-                nc.sync.dma_start(out=out[:, g * GT : (g + 1) * GT, cols], in_=o[:, :, cols])
+                    nc.sync.dma_start(out=out[:, n0 : n0 + GT, :], in_=o[:])
+            elif unit < UNITS - 1:
+                nc.sync.dma_start(out=out[:, n0 : n0 + GT, cols], in_=o[:, :, cols])
 
         wraw = const.tile([P, HEADS, 4, DH], BF16)
         bz = const.tile([P, P], BF16)
         nc.vector.memset(bz[:], 0.0)
-        load_x(0, 2)
+        x0 = loads.tile([P, GT, HEADS, K], BF16, name="x0", tag="x")
+        x_tiles[0] = x0
+        nc.sync.dma_start(out=x0[:, :, 0, :], in_=out_t[:, 0:GT, 0, :])
+        nc.sync.dma_start(
+            out=wraw[:].rearrange("q h (u e) c -> q h u (e c)", u=2),
+            in_=out_w.rearrange("h (u q e) c -> q h u (e c)", u=2, q=P, e=2),
+        )
+        nc.sync.dma_start(out=x0[:, :, 1, :], in_=out_t[:, 0:GT, 1, :])
         nc.sync.dma_start(out=bz[0:4, :], in_=out_b.rearrange("(j m) -> j m", j=4))
-        load_x(1, 1)
+        load_x(1)
         load_sv(0)
         for g in range(2, 4):
-            load_x(g, 1)
+            load_x(g)
             load_sv(g - 1)
 
-
         wg = const.tile([P, HEADS, DH, 4], BF16, align_bytes=64)
-        nc.vector.tensor_copy(out=wg[:], in_=wraw[:].rearrange("q h t c -> q h c t"))
         w_codes = const.tile([P, HEADS * DH], U32, align_bytes=64)
         w_scales = const.tile([P, HEADS * DH], U8, align_bytes=64)
-        nc.vector.quantize_mx(
-            out=w_codes[:].bitcast(FP8X4),
-            scales=w_scales[:],
-            in_=wg[:].rearrange("q h c t -> q (h c t)"),
-        )
+        for h in range(HEADS):
+            nc.vector.tensor_copy(out=wg[:, h], in_=wraw[:, h].rearrange("q t c -> q c t"))
+            nc.vector.quantize_mx(
+                out=w_codes[:, h * DH : (h + 1) * DH].bitcast(FP8X4),
+                scales=w_scales[:, h * DH : (h + 1) * DH],
+                in_=wg[:, h].rearrange("q c t -> q (c t)"),
+            )
         bzf = const.tile([P, P], F32)
         bias_col = const.tile([P, 4], F32)
 
@@ -221,23 +218,20 @@ def tile_implicitrelationencoder_pb_t_kernel(tc, out_t, out_w, out_b, self_feat,
             if step % HEADS == 0:
                 g = step // HEADS + 4
                 if g < GROUPS:
-                    load_x(g, 1)
+                    load_x(g)
                 if g - 1 < GROUPS:
                     load_sv(g - 1)
-            if 0 <= step < UNITS:
+            if step < UNITS:
                 transpose_in(step)
-            if 0 <= step - 1 < UNITS:
-                quantise(step - 1)
             if step == 1:
                 nc.vector.tensor_copy(out=bzf[:], in_=bz[:])
                 bt = psum_b.tile([P, P], F32, name="bt", tag="tb")
                 nc.tensor.transpose(bt[:], bzf[:], ident[:])
                 nc.vector.tensor_copy(out=bias_col[:], in_=bt[:, 0:4])
             if 0 <= step - 1 < UNITS:
+                quantise(step - 1)
                 multiply(step - 1)
             if 0 <= step - 2 < UNITS:
                 transpose_back(step - 2)
             if 0 <= step - 3 < UNITS:
                 finish(step - 3)
-            if 0 <= step - 3 < UNITS:
-                store(step - 3)

@@ -24,6 +24,9 @@ NCOL = GT * P
 FLOPS = 2 * P * NOBJ * HEADS * K * DH
 UNITS = GROUPS * HEADS
 FIRST_PE_ADD = 5
+X_CHUNKS = [[0], [1], [2], [3, 4], [5, 6], [7, 8]]
+SV_CHUNKS = [[0], [1], [2], [3, 4], [5, 6], [7, 8]]
+OUT_CHUNKS = [[0], [1, 2], [3, 4], [5, 6], [7], [8]]
 
 
 def pe_adds(unit, pair):
@@ -34,11 +37,11 @@ def tile_implicitrelationencoder_pb_t_kernel(tc, out_t, out_w, out_b, self_feat,
     nc = tc.nc
     with ExitStack() as ctx:
         const = ctx.enter_context(tc.tile_pool(name="const", bufs=1))
-        loads = ctx.enter_context(tc.tile_pool(name="loads", bufs=6))
+        loads = ctx.enter_context(tc.tile_pool(name="loads", bufs=1))
         gpool = ctx.enter_context(tc.tile_pool(name="gpool", bufs=2))
         cpool = ctx.enter_context(tc.tile_pool(name="cpool", bufs=2))
         upool = ctx.enter_context(tc.tile_pool(name="upool", bufs=4))
-        outs = ctx.enter_context(tc.tile_pool(name="outs", bufs=5))
+        outs = ctx.enter_context(tc.tile_pool(name="outs", bufs=3))
         psum_t = ctx.enter_context(tc.psum_pool(name="psum_t", bufs=2))
         psum_a = ctx.enter_context(tc.psum_pool(name="psum_a", bufs=2))
         psum_b = ctx.enter_context(tc.psum_pool(name="psum_b", bufs=4))
@@ -58,23 +61,37 @@ def tile_implicitrelationencoder_pb_t_kernel(tc, out_t, out_w, out_b, self_feat,
         u_tiles = {}
         tb_tiles = {}
 
-        def load_x(g):
-            x = loads.tile([P, GT, HEADS, K], BF16, name="x%d" % g, tag="x")
-            nc.sync.dma_start(out=x[:], in_=out_t[:, g * GT : (g + 1) * GT])
-            x_tiles[g] = x
+        def load_x(chunk):
+            g0 = chunk[0]
+            rows = len(chunk) * GT
+            x = loads.tile([P, rows, HEADS, K], BF16, name="x%d" % g0)
+            for i, g in enumerate(chunk):
+                x_tiles[g] = x[:, i * GT : (i + 1) * GT]
+            if g0 == 0:
+                nc.sync.dma_start(out=x[:, :, 0, :], in_=out_t[:, 0:GT, 0, :])
+                nc.sync.dma_start(
+                    out=wraw[:].rearrange("q h (u e) c -> q h u (e c)", u=2),
+                    in_=out_w.rearrange("h (u q e) c -> q h u (e c)", u=2, q=P, e=2),
+                )
+                nc.sync.dma_start(out=x[:, :, 1, :], in_=out_t[:, 0:GT, 1, :])
+                nc.sync.dma_start(out=bz[0:4, :], in_=out_b.rearrange("(j m) -> j m", j=4))
+            else:
+                nc.sync.dma_start(out=x[:], in_=out_t[:, g0 * GT : g0 * GT + rows])
 
-        def load_sv(g):
-            n0 = g * GT
-            s = loads.tile([P, GT, D], BF16, name="s%d" % g, tag="s")
-            nc.sync.dma_start(out=s[:], in_=self_feat[:, n0 : n0 + GT, :])
-            s_tiles[g] = s
-            v = loads.tile([P, GT, D], BF16, name="v%d" % g, tag="v")
-            nc.sync.dma_start(out=v[:], in_=vis[:, n0 : n0 + GT, :])
-            v_tiles[g] = v
+        def load_sv(chunk):
+            g0 = chunk[0]
+            rows = len(chunk) * GT
+            s = loads.tile([P, rows, D], BF16, name="s%d" % g0)
+            nc.sync.dma_start(out=s[:], in_=self_feat[:, g0 * GT : g0 * GT + rows, :])
+            v = loads.tile([P, rows, D], BF16, name="v%d" % g0)
+            nc.sync.dma_start(out=v[:], in_=vis[:, g0 * GT : g0 * GT + rows, :])
+            for i, g in enumerate(chunk):
+                s_tiles[g] = s[:, i * GT : (i + 1) * GT]
+                v_tiles[g] = v[:, i * GT : (i + 1) * GT]
 
         def transpose_in(unit):
             g, h = divmod(unit, HEADS)
-            xw = x_tiles[g][:].rearrange("p n h k -> p (n h k)").bitcast(F32)
+            xw = x_tiles[g].rearrange("p n h k -> p (n h k)").bitcast(F32)
             grouped = gpool.tile([P, NCOL * 4], BF16, align_bytes=64, name="grouped", tag="grouped")
             gw = grouped[:].bitcast(F32)
             for pair in range(2):
@@ -151,9 +168,12 @@ def tile_implicitrelationencoder_pb_t_kernel(tc, out_t, out_w, out_b, self_feat,
 
         def finish(unit):
             g, h = divmod(unit, HEADS)
-            if h == 0:
-                o_tiles[g] = outs.tile([P, GT, D], F32, name="o", tag="o")
-            o = o_tiles[g]
+            chunk = [c for c in OUT_CHUNKS if g in c][0]
+            if h == 0 and g == chunk[0]:
+                whole = outs.tile([P, len(chunk) * GT, D], F32, name="o", tag="o")
+                for i, gg in enumerate(chunk):
+                    o_tiles[gg] = (whole[:, i * GT : (i + 1) * GT], whole)
+            o, whole = o_tiles[g]
             v = v_tiles[g]
             cols = slice(h * DH, (h + 1) * DH)
             n0 = g * GT
@@ -178,28 +198,27 @@ def tile_implicitrelationencoder_pb_t_kernel(tc, out_t, out_w, out_b, self_feat,
                     op0=ALU.max, op1=ALU.add,
                 )
             if g < GROUPS - 1:
-                if h == HEADS - 1:
-                    nc.sync.dma_start(out=out[:, n0 : n0 + GT, :], in_=o[:])
+                if h == HEADS - 1 and g == chunk[-1]:
+                    nc.sync.dma_start(out=out[:, chunk[0] * GT : (g + 1) * GT, :], in_=whole[:])
             elif unit < UNITS - 1:
                 nc.sync.dma_start(out=out[:, n0 : n0 + GT, cols], in_=o[:, :, cols])
 
         wraw = const.tile([P, HEADS, 4, DH], BF16)
         bz = const.tile([P, P], BF16)
         nc.vector.memset(bz[:], 0.0)
-        x0 = loads.tile([P, GT, HEADS, K], BF16, name="x0", tag="x")
-        x_tiles[0] = x0
-        nc.sync.dma_start(out=x0[:, :, 0, :], in_=out_t[:, 0:GT, 0, :])
-        nc.sync.dma_start(
-            out=wraw[:].rearrange("q h (u e) c -> q h u (e c)", u=2),
-            in_=out_w.rearrange("h (u q e) c -> q h u (e c)", u=2, q=P, e=2),
+        load_plan = sorted(
+            [(2 * c[0] - 8, 0, c) for c in X_CHUNKS] + [(2 * c[0] - 5, 1, c) for c in SV_CHUNKS]
         )
-        nc.sync.dma_start(out=x0[:, :, 1, :], in_=out_t[:, 0:GT, 1, :])
-        nc.sync.dma_start(out=bz[0:4, :], in_=out_b.rearrange("(j m) -> j m", j=4))
-        load_x(1)
-        load_sv(0)
-        for g in range(2, 4):
-            load_x(g)
-            load_sv(g - 1)
+
+        def trigger_loads(step):
+            for when, kind, chunk in load_plan:
+                if when == step or (step == 0 and when < 0):
+                    if kind == 0:
+                        load_x(chunk)
+                    else:
+                        load_sv(chunk)
+
+        trigger_loads(0)
 
         wg = const.tile([P, HEADS, DH, 4], BF16, align_bytes=64)
         w_codes = const.tile([P, HEADS * DH], U32, align_bytes=64)
@@ -215,12 +234,8 @@ def tile_implicitrelationencoder_pb_t_kernel(tc, out_t, out_w, out_b, self_feat,
         bias_col = const.tile([P, 4], F32)
 
         for step in range(UNITS + 3):
-            if step % HEADS == 0:
-                g = step // HEADS + 4
-                if g < GROUPS:
-                    load_x(g)
-                if g - 1 < GROUPS:
-                    load_sv(g - 1)
+            if step > 0:
+                trigger_loads(step)
             if step < UNITS:
                 transpose_in(step)
             if step == 1:

@@ -16,17 +16,29 @@ NOBJ = 36
 HEADS = 2
 K = 512
 DH = 256
-D = 512
-GT = 4
-GROUPS = NOBJ // GT
-NCOL = GT * P
+D = HEADS * DH
+PANELS = DH // P
+PACK = 4
+QUAD = 4
+QUADS = NOBJ // QUAD
+NCOL = QUAD * P
+UNITS = QUADS * HEADS
+PAIRS = QUAD // 2
 
 FLOPS = 2 * P * NOBJ * HEADS * K * DH
-UNITS = GROUPS * HEADS
+
+MULTIPLY_LAG = 1
+BACK_LAG = 2
+FINISH_LAG = 3
+
 FIRST_PE_ADD = 5
+
 X_CHUNKS = [[0], [1], [2], [3, 4], [5, 6], [7, 8]]
 SV_CHUNKS = [[0], [1], [2], [3, 4], [5, 6], [7, 8]]
 OUT_CHUNKS = [[0], [1, 2], [3, 4], [5, 6], [7], [8]]
+
+X_LEAD = 8
+SV_LEAD = 5
 
 
 def pe_adds(unit, pair):
@@ -62,46 +74,49 @@ def tile_implicitrelationencoder_pb_t_kernel(tc, out_t, out_w, out_b, self_feat,
         tb_tiles = {}
 
         def load_x(chunk):
-            g0 = chunk[0]
-            rows = len(chunk) * GT
-            x = loads.tile([P, rows, HEADS, K], BF16, name="x%d" % g0)
-            for i, g in enumerate(chunk):
-                x_tiles[g] = x[:, i * GT : (i + 1) * GT]
-            if g0 == 0:
-                nc.sync.dma_start(out=x[:, :, 0, :], in_=out_t[:, 0:GT, 0, :])
+            first = chunk[0]
+            n_tiles = len(chunk) * QUAD
+            x = loads.tile([P, n_tiles, HEADS, K], BF16, name="x%d" % first)
+            for i, quad in enumerate(chunk):
+                x_tiles[quad] = x[:, i * QUAD : (i + 1) * QUAD]
+            if first == 0:
+                nc.sync.dma_start(out=x[:, :, 0, :], in_=out_t[:, 0:QUAD, 0, :])
                 nc.sync.dma_start(
                     out=wraw[:].rearrange("q h (u e) c -> q h u (e c)", u=2),
                     in_=out_w.rearrange("h (u q e) c -> q h u (e c)", u=2, q=P, e=2),
                 )
-                nc.sync.dma_start(out=x[:, :, 1, :], in_=out_t[:, 0:GT, 1, :])
-                nc.sync.dma_start(out=bz[0:4, :], in_=out_b.rearrange("(j m) -> j m", j=4))
+                nc.sync.dma_start(out=x[:, :, 1, :], in_=out_t[:, 0:QUAD, 1, :])
+                nc.sync.dma_start(out=bias_rows[0 : D // P, :], in_=out_b.rearrange("(j m) -> j m", j=D // P))
             else:
-                nc.sync.dma_start(out=x[:], in_=out_t[:, g0 * GT : g0 * GT + rows])
+                nc.sync.dma_start(out=x[:], in_=out_t[:, first * QUAD : first * QUAD + n_tiles])
 
         def load_sv(chunk):
-            g0 = chunk[0]
-            rows = len(chunk) * GT
-            s = loads.tile([P, rows, D], BF16, name="s%d" % g0)
-            nc.sync.dma_start(out=s[:], in_=self_feat[:, g0 * GT : g0 * GT + rows, :])
-            v = loads.tile([P, rows, D], BF16, name="v%d" % g0)
-            nc.sync.dma_start(out=v[:], in_=vis[:, g0 * GT : g0 * GT + rows, :])
-            for i, g in enumerate(chunk):
-                s_tiles[g] = s[:, i * GT : (i + 1) * GT]
-                v_tiles[g] = v[:, i * GT : (i + 1) * GT]
+            first = chunk[0]
+            n_tiles = len(chunk) * QUAD
+            s = loads.tile([P, n_tiles, D], BF16, name="s%d" % first)
+            nc.sync.dma_start(out=s[:], in_=self_feat[:, first * QUAD : first * QUAD + n_tiles, :])
+            v = loads.tile([P, n_tiles, D], BF16, name="v%d" % first)
+            nc.sync.dma_start(out=v[:], in_=vis[:, first * QUAD : first * QUAD + n_tiles, :])
+            for i, quad in enumerate(chunk):
+                s_tiles[quad] = s[:, i * QUAD : (i + 1) * QUAD]
+                v_tiles[quad] = v[:, i * QUAD : (i + 1) * QUAD]
 
         def transpose_in(unit):
-            g, h = divmod(unit, HEADS)
-            xw = x_tiles[g].rearrange("p n h k -> p (n h k)").bitcast(F32)
-            grouped = gpool.tile([P, NCOL * 4], BF16, align_bytes=64, name="grouped", tag="grouped")
-            gw = grouped[:].bitcast(F32)
-            for pair in range(2):
+            quad, h = divmod(unit, HEADS)
+            x_f32 = x_tiles[quad].rearrange("p n h k -> p (n h k)").bitcast(F32)
+            grouped = gpool.tile([P, NCOL * PACK], BF16, align_bytes=64, name="grouped", tag="grouped")
+            grouped_f32 = grouped[:].bitcast(F32)
+            bank_cols = 2 * 2 * P
+            for pair in range(PAIRS):
                 xt = psum_t.tile([P, 2, 2, P], F32, name="xt", tag="xt")
                 for n2 in range(2):
                     for u in range(2):
-                        c0 = ((pair * 2 + n2) * HEADS + h) * 256 + u * P
-                        nc.tensor.transpose(xt[:, n2, u, :], xw[:, c0 : c0 + P], ident[:])
+                        c0 = ((pair * 2 + n2) * HEADS + h) * (K // 2) + u * P
+                        nc.tensor.transpose(xt[:, n2, u, :], x_f32[:, c0 : c0 + P], ident[:])
                 nc.scalar.copy(
-                    out=gw[:, pair * 512 : (pair + 1) * 512].rearrange("q (n b u) -> q n b u", n=2, u=2),
+                    out=grouped_f32[:, pair * bank_cols : (pair + 1) * bank_cols].rearrange(
+                        "q (n b u) -> q n b u", n=2, u=2
+                    ),
                     in_=xt[:].rearrange("q n u b -> q n b u"),
                 )
             grouped_tiles[unit] = grouped
@@ -115,14 +130,14 @@ def tile_implicitrelationencoder_pb_t_kernel(tc, out_t, out_w, out_b, self_feat,
         def multiply(unit):
             h = unit % HEADS
             codes, scales = code_tiles[unit]
-            us = []
-            for j in range(2):
-                cb = h * 2 + j
+            biased = []
+            for j in range(PANELS):
+                panel = h * PANELS + j
                 acc = psum_a.tile([P, NCOL], F32, name="acc", tag="acc")
                 nc.tensor.matmul_mx(
                     out=acc[:],
-                    lhsT=w_codes[:, cb * P : (cb + 1) * P].bitcast(FP8X4),
-                    lhsT_scale=w_scales[:, cb * P : (cb + 1) * P],
+                    lhsT=w_codes[:, panel * P : (panel + 1) * P].bitcast(FP8X4),
+                    lhsT_scale=w_scales[:, panel * P : (panel + 1) * P],
                     rhs=codes[:].bitcast(FP8X4),
                     rhs_scale=scales[:],
                     start=True,
@@ -130,16 +145,16 @@ def tile_implicitrelationencoder_pb_t_kernel(tc, out_t, out_w, out_b, self_feat,
                 )
                 u_sb = upool.tile([P, NCOL], F32, name="u_sb", tag="u")
                 nc.scalar.activation(
-                    out=u_sb[:], in_=acc[:], func=ACT.Identity, bias=bias_col[:, cb : cb + 1], scale=1.0
+                    out=u_sb[:], in_=acc[:], func=ACT.Identity, bias=bias_col[:, panel : panel + 1], scale=1.0
                 )
-                us.append(u_sb)
-            u_tiles[unit] = us
+                biased.append(u_sb)
+            u_tiles[unit] = biased
 
         def transpose_back(unit):
-            g, h = divmod(unit, HEADS)
-            us = u_tiles[unit]
-            tbs = []
-            for pair in range(2):
+            quad, h = divmod(unit, HEADS)
+            biased = u_tiles[unit]
+            banks = []
+            for pair in range(PAIRS):
                 tb = psum_b.tile([P, 2, DH], F32, name="tb", tag="tb")
                 for n2 in range(2):
                     n = pair * 2 + n2
@@ -147,80 +162,84 @@ def tile_implicitrelationencoder_pb_t_kernel(tc, out_t, out_w, out_b, self_feat,
                         nc.tensor.matmul(
                             out=tb[:, n2, :],
                             lhsT=ident_bf[:],
-                            rhs=s_tiles[g][:, n, h * DH : (h + 1) * DH],
+                            rhs=s_tiles[quad][:, n, h * DH : (h + 1) * DH],
                             start=True,
                             stop=False,
                         )
-                        for j in range(2):
+                        for j in range(PANELS):
                             nc.tensor.matmul(
                                 out=tb[:, n2, j * P : (j + 1) * P],
-                                lhsT=us[j][:, n * P : (n + 1) * P],
+                                lhsT=biased[j][:, n * P : (n + 1) * P],
                                 rhs=ident[:],
                                 is_transpose=True,
                                 start=False,
-                                stop=(j == 1),
+                                stop=(j == PANELS - 1),
                             )
                     else:
-                        for j in range(2):
-                            nc.tensor.transpose(tb[:, n2, j * P : (j + 1) * P], us[j][:, n * P : (n + 1) * P], ident[:])
-                tbs.append(tb)
-            tb_tiles[unit] = tbs
+                        for j in range(PANELS):
+                            nc.tensor.transpose(
+                                tb[:, n2, j * P : (j + 1) * P], biased[j][:, n * P : (n + 1) * P], ident[:]
+                            )
+                banks.append(tb)
+            tb_tiles[unit] = banks
 
         def finish(unit):
-            g, h = divmod(unit, HEADS)
-            chunk = [c for c in OUT_CHUNKS if g in c][0]
-            if h == 0 and g == chunk[0]:
-                whole = outs.tile([P, len(chunk) * GT, D], F32, name="o", tag="o")
-                for i, gg in enumerate(chunk):
-                    o_tiles[gg] = (whole[:, i * GT : (i + 1) * GT], whole)
-            o, whole = o_tiles[g]
-            v = v_tiles[g]
+            quad, h = divmod(unit, HEADS)
+            chunk = [c for c in OUT_CHUNKS if quad in c][0]
+            if h == 0 and quad == chunk[0]:
+                whole = outs.tile([P, len(chunk) * QUAD, D], F32, name="o", tag="o")
+                for i, member in enumerate(chunk):
+                    o_tiles[member] = (whole[:, i * QUAD : (i + 1) * QUAD], whole)
+            o, whole = o_tiles[quad]
+            v = v_tiles[quad]
             cols = slice(h * DH, (h + 1) * DH)
-            n0 = g * GT
-            plain = [pair for pair in range(2) if not pe_adds(unit, pair)]
-            for pair in range(2):
-                rows = slice(pair * 2, pair * 2 + 2)
+            n0 = quad * QUAD
+            for pair in range(PAIRS):
+                both = slice(pair * 2, pair * 2 + 2)
                 if pe_adds(unit, pair):
                     nc.vector.scalar_tensor_tensor(
-                        out=o[:, rows, cols], in0=tb_tiles[unit][pair][:], scalar=0.0, in1=v[:, rows, cols],
+                        out=o[:, both, cols], in0=tb_tiles[unit][pair][:], scalar=0.0, in1=v[:, both, cols],
                         op0=ALU.max, op1=ALU.add,
                     )
                     if unit == UNITS - 1:
-                        nc.sync.dma_start(out=out[:, n0 + pair * 2 : n0 + pair * 2 + 2, cols], in_=o[:, rows, cols])
+                        nc.sync.dma_start(out=out[:, n0 + pair * 2 : n0 + pair * 2 + 2, cols], in_=o[:, both, cols])
                 else:
                     nc.vector.tensor_tensor(
-                        out=o[:, rows, cols], in0=tb_tiles[unit][pair][:], in1=s_tiles[g][:, rows, cols], op=ALU.add
+                        out=o[:, both, cols], in0=tb_tiles[unit][pair][:], in1=s_tiles[quad][:, both, cols],
+                        op=ALU.add,
                     )
-            if plain:
-                rest = slice(plain[0] * 2, GT)
+            vector_pairs = [pair for pair in range(PAIRS) if not pe_adds(unit, pair)]
+            if vector_pairs:
+                rest = slice(vector_pairs[0] * 2, QUAD)
                 nc.vector.scalar_tensor_tensor(
                     out=o[:, rest, cols], in0=o[:, rest, cols], scalar=0.0, in1=v[:, rest, cols],
                     op0=ALU.max, op1=ALU.add,
                 )
-            if g < GROUPS - 1:
-                if h == HEADS - 1 and g == chunk[-1]:
-                    nc.sync.dma_start(out=out[:, chunk[0] * GT : (g + 1) * GT, :], in_=whole[:])
+            if quad < QUADS - 1:
+                if h == HEADS - 1 and quad == chunk[-1]:
+                    nc.sync.dma_start(out=out[:, chunk[0] * QUAD : (quad + 1) * QUAD, :], in_=whole[:])
             elif unit < UNITS - 1:
-                nc.sync.dma_start(out=out[:, n0 : n0 + GT, cols], in_=o[:, :, cols])
+                nc.sync.dma_start(out=out[:, n0 : n0 + QUAD, cols], in_=o[:, :, cols])
 
-        wraw = const.tile([P, HEADS, 4, DH], BF16)
-        bz = const.tile([P, P], BF16)
-        nc.vector.memset(bz[:], 0.0)
+        wraw = const.tile([P, HEADS, PACK, DH], BF16)
+        bias_rows = const.tile([P, P], BF16)
+        nc.vector.memset(bias_rows[:], 0.0)
+
         load_plan = sorted(
-            [(2 * c[0] - 8, 0, c) for c in X_CHUNKS] + [(2 * c[0] - 5, 1, c) for c in SV_CHUNKS]
+            [(2 * c[0] - X_LEAD, 0, c) for c in X_CHUNKS] + [(2 * c[0] - SV_LEAD, 1, c) for c in SV_CHUNKS]
         )
 
         def trigger_loads(step):
-            for when, kind, chunk in load_plan:
-                if when == step or (step == 0 and when < 0):
-                    if kind == 0:
-                        load_x(chunk)
-                    else:
+            for due, is_sv, chunk in load_plan:
+                if due == step or (step == 0 and due < 0):
+                    if is_sv:
                         load_sv(chunk)
+                    else:
+                        load_x(chunk)
 
         trigger_loads(0)
 
-        wg = const.tile([P, HEADS, DH, 4], BF16, align_bytes=64)
+        wg = const.tile([P, HEADS, DH, PACK], BF16, align_bytes=64)
         w_codes = const.tile([P, HEADS * DH], U32, align_bytes=64)
         w_scales = const.tile([P, HEADS * DH], U8, align_bytes=64)
         for h in range(HEADS):
@@ -230,23 +249,26 @@ def tile_implicitrelationencoder_pb_t_kernel(tc, out_t, out_w, out_b, self_feat,
                 scales=w_scales[:, h * DH : (h + 1) * DH],
                 in_=wg[:, h].rearrange("q c t -> q (c t)"),
             )
-        bzf = const.tile([P, P], F32)
-        bias_col = const.tile([P, 4], F32)
+        bias_rows_f32 = const.tile([P, P], F32)
+        bias_col = const.tile([P, D // P], F32)
 
-        for step in range(UNITS + 3):
+        def bias_to_partitions():
+            nc.vector.tensor_copy(out=bias_rows_f32[:], in_=bias_rows[:])
+            bt = psum_b.tile([P, P], F32, name="bt", tag="tb")
+            nc.tensor.transpose(bt[:], bias_rows_f32[:], ident[:])
+            nc.vector.tensor_copy(out=bias_col[:], in_=bt[:, 0 : D // P])
+
+        for step in range(UNITS + FINISH_LAG):
             if step > 0:
                 trigger_loads(step)
             if step < UNITS:
                 transpose_in(step)
-            if step == 1:
-                nc.vector.tensor_copy(out=bzf[:], in_=bz[:])
-                bt = psum_b.tile([P, P], F32, name="bt", tag="tb")
-                nc.tensor.transpose(bt[:], bzf[:], ident[:])
-                nc.vector.tensor_copy(out=bias_col[:], in_=bt[:, 0:4])
-            if 0 <= step - 1 < UNITS:
-                quantise(step - 1)
-                multiply(step - 1)
-            if 0 <= step - 2 < UNITS:
-                transpose_back(step - 2)
-            if 0 <= step - 3 < UNITS:
-                finish(step - 3)
+            if step == MULTIPLY_LAG:
+                bias_to_partitions()
+            if 0 <= step - MULTIPLY_LAG < UNITS:
+                quantise(step - MULTIPLY_LAG)
+                multiply(step - MULTIPLY_LAG)
+            if 0 <= step - BACK_LAG < UNITS:
+                transpose_back(step - BACK_LAG)
+            if 0 <= step - FINISH_LAG < UNITS:
+                finish(step - FINISH_LAG)

from contextlib import ExitStack

import concourse.mybir as mybir
from concourse.masks import make_identity

F32 = mybir.dt.float32
BF16 = mybir.dt.bfloat16
U32 = mybir.dt.uint32
U8 = mybir.dt.uint8
FP8X4 = mybir.dt.float8_e4m3fn_x4
ALU = mybir.AluOpType
ACT = mybir.ActivationFunctionType

P = 128
NOBJ = 36
HEADS = 2
K = 512
DH = 256
D = HEADS * DH
PANELS = DH // P
PACK = 4
QUAD = 4
QUADS = NOBJ // QUAD
NCOL = QUAD * P
UNITS = QUADS * HEADS
PAIRS = QUAD // 2

FLOPS = 2 * P * NOBJ * HEADS * K * DH

MULTIPLY_LAG = 1
BACK_LAG = 2
FINISH_LAG = 3

FIRST_PE_ADD = 5

X_CHUNKS = [[0], [1], [2], [3, 4], [5, 6], [7, 8]]
SV_CHUNKS = [[0], [1], [2], [3, 4], [5, 6], [7, 8]]
OUT_CHUNKS = [[0], [1, 2], [3, 4], [5, 6], [7], [8]]

X_LEAD = 8
SV_LEAD = 5


def pe_adds(unit, pair):
    return (pair == 0 and unit >= FIRST_PE_ADD) or unit == UNITS - 1


def tile_implicitrelationencoder_pb_t_kernel(tc, out_t, out_w, out_b, self_feat, vis, out):
    nc = tc.nc
    with ExitStack() as ctx:
        const = ctx.enter_context(tc.tile_pool(name="const", bufs=1))
        loads = ctx.enter_context(tc.tile_pool(name="loads", bufs=1))
        gpool = ctx.enter_context(tc.tile_pool(name="gpool", bufs=2))
        cpool = ctx.enter_context(tc.tile_pool(name="cpool", bufs=2))
        upool = ctx.enter_context(tc.tile_pool(name="upool", bufs=4))
        outs = ctx.enter_context(tc.tile_pool(name="outs", bufs=3))
        psum_t = ctx.enter_context(tc.psum_pool(name="psum_t", bufs=2))
        psum_a = ctx.enter_context(tc.psum_pool(name="psum_a", bufs=2))
        psum_b = ctx.enter_context(tc.psum_pool(name="psum_b", bufs=4))
        ctx.enter_context(tc.manual_schedule())

        ident = const.tile([P, P], F32)
        make_identity(nc, ident[:])
        ident_bf = const.tile([P, P], BF16)
        make_identity(nc, ident_bf[:])

        x_tiles = {}
        s_tiles = {}
        v_tiles = {}
        o_tiles = {}
        grouped_tiles = {}
        code_tiles = {}
        u_tiles = {}
        tb_tiles = {}

        def load_x(chunk):
            first = chunk[0]
            n_tiles = len(chunk) * QUAD
            x = loads.tile([P, n_tiles, HEADS, K], BF16, name="x%d" % first)
            for i, quad in enumerate(chunk):
                x_tiles[quad] = x[:, i * QUAD : (i + 1) * QUAD]
            if first == 0:
                nc.sync.dma_start(out=x[:, :, 0, :], in_=out_t[:, 0:QUAD, 0, :])
                nc.sync.dma_start(
                    out=wraw[:].rearrange("q h (u e) c -> q h u (e c)", u=2),
                    in_=out_w.rearrange("h (u q e) c -> q h u (e c)", u=2, q=P, e=2),
                )
                nc.sync.dma_start(out=x[:, :, 1, :], in_=out_t[:, 0:QUAD, 1, :])
                nc.sync.dma_start(out=bias_rows[0 : D // P, :], in_=out_b.rearrange("(j m) -> j m", j=D // P))
            else:
                nc.sync.dma_start(out=x[:], in_=out_t[:, first * QUAD : first * QUAD + n_tiles])

        def load_sv(chunk):
            first = chunk[0]
            n_tiles = len(chunk) * QUAD
            s = loads.tile([P, n_tiles, D], BF16, name="s%d" % first)
            nc.sync.dma_start(out=s[:], in_=self_feat[:, first * QUAD : first * QUAD + n_tiles, :])
            v = loads.tile([P, n_tiles, D], BF16, name="v%d" % first)
            nc.sync.dma_start(out=v[:], in_=vis[:, first * QUAD : first * QUAD + n_tiles, :])
            for i, quad in enumerate(chunk):
                s_tiles[quad] = s[:, i * QUAD : (i + 1) * QUAD]
                v_tiles[quad] = v[:, i * QUAD : (i + 1) * QUAD]

        def transpose_in(unit):
            quad, h = divmod(unit, HEADS)
            x_f32 = x_tiles[quad].rearrange("p n h k -> p (n h k)").bitcast(F32)
            grouped = gpool.tile([P, NCOL * PACK], BF16, align_bytes=64, name="grouped", tag="grouped")
            grouped_f32 = grouped[:].bitcast(F32)
            bank_cols = 2 * 2 * P
            for pair in range(PAIRS):
                xt = psum_t.tile([P, 2, 2, P], F32, name="xt", tag="xt")
                for n2 in range(2):
                    for u in range(2):
                        c0 = ((pair * 2 + n2) * HEADS + h) * (K // 2) + u * P
                        nc.tensor.transpose(xt[:, n2, u, :], x_f32[:, c0 : c0 + P], ident[:])
                nc.scalar.copy(
                    out=grouped_f32[:, pair * bank_cols : (pair + 1) * bank_cols].rearrange(
                        "q (n b u) -> q n b u", n=2, u=2
                    ),
                    in_=xt[:].rearrange("q n u b -> q n b u"),
                )
            grouped_tiles[unit] = grouped

        def quantise(unit):
            codes = cpool.tile([P, NCOL], U32, align_bytes=64, name="codes", tag="codes")
            scales = cpool.tile([P, NCOL], U8, align_bytes=64, name="scales", tag="scales")
            nc.vector.quantize_mx(out=codes[:].bitcast(FP8X4), scales=scales[:], in_=grouped_tiles[unit][:])
            code_tiles[unit] = (codes, scales)

        def multiply(unit):
            h = unit % HEADS
            codes, scales = code_tiles[unit]
            biased = []
            for j in range(PANELS):
                panel = h * PANELS + j
                acc = psum_a.tile([P, NCOL], F32, name="acc", tag="acc")
                nc.tensor.matmul_mx(
                    out=acc[:],
                    lhsT=w_codes[:, panel * P : (panel + 1) * P].bitcast(FP8X4),
                    lhsT_scale=w_scales[:, panel * P : (panel + 1) * P],
                    rhs=codes[:].bitcast(FP8X4),
                    rhs_scale=scales[:],
                    start=True,
                    stop=True,
                )
                u_sb = upool.tile([P, NCOL], F32, name="u_sb", tag="u")
                nc.scalar.activation(
                    out=u_sb[:], in_=acc[:], func=ACT.Identity, bias=bias_col[:, panel : panel + 1], scale=1.0
                )
                biased.append(u_sb)
            u_tiles[unit] = biased

        def transpose_back(unit):
            quad, h = divmod(unit, HEADS)
            biased = u_tiles[unit]
            banks = []
            for pair in range(PAIRS):
                tb = psum_b.tile([P, 2, DH], F32, name="tb", tag="tb")
                for n2 in range(2):
                    n = pair * 2 + n2
                    if pe_adds(unit, pair):
                        nc.tensor.matmul(
                            out=tb[:, n2, :],
                            lhsT=ident_bf[:],
                            rhs=s_tiles[quad][:, n, h * DH : (h + 1) * DH],
                            start=True,
                            stop=False,
                        )
                        for j in range(PANELS):
                            nc.tensor.matmul(
                                out=tb[:, n2, j * P : (j + 1) * P],
                                lhsT=biased[j][:, n * P : (n + 1) * P],
                                rhs=ident[:],
                                is_transpose=True,
                                start=False,
                                stop=(j == PANELS - 1),
                            )
                    else:
                        for j in range(PANELS):
                            nc.tensor.transpose(
                                tb[:, n2, j * P : (j + 1) * P], biased[j][:, n * P : (n + 1) * P], ident[:]
                            )
                banks.append(tb)
            tb_tiles[unit] = banks

        def finish(unit):
            quad, h = divmod(unit, HEADS)
            chunk = [c for c in OUT_CHUNKS if quad in c][0]
            if h == 0 and quad == chunk[0]:
                whole = outs.tile([P, len(chunk) * QUAD, D], F32, name="o", tag="o")
                for i, member in enumerate(chunk):
                    o_tiles[member] = (whole[:, i * QUAD : (i + 1) * QUAD], whole)
            o, whole = o_tiles[quad]
            v = v_tiles[quad]
            cols = slice(h * DH, (h + 1) * DH)
            n0 = quad * QUAD
            for pair in range(PAIRS):
                both = slice(pair * 2, pair * 2 + 2)
                if pe_adds(unit, pair):
                    nc.vector.scalar_tensor_tensor(
                        out=o[:, both, cols], in0=tb_tiles[unit][pair][:], scalar=0.0, in1=v[:, both, cols],
                        op0=ALU.max, op1=ALU.add,
                    )
                    if unit == UNITS - 1:
                        nc.sync.dma_start(out=out[:, n0 + pair * 2 : n0 + pair * 2 + 2, cols], in_=o[:, both, cols])
                else:
                    nc.vector.tensor_tensor(
                        out=o[:, both, cols], in0=tb_tiles[unit][pair][:], in1=s_tiles[quad][:, both, cols],
                        op=ALU.add,
                    )
            vector_pairs = [pair for pair in range(PAIRS) if not pe_adds(unit, pair)]
            if vector_pairs:
                rest = slice(vector_pairs[0] * 2, QUAD)
                nc.vector.scalar_tensor_tensor(
                    out=o[:, rest, cols], in0=o[:, rest, cols], scalar=0.0, in1=v[:, rest, cols],
                    op0=ALU.max, op1=ALU.add,
                )
            if quad < QUADS - 1:
                if h == HEADS - 1 and quad == chunk[-1]:
                    nc.sync.dma_start(out=out[:, chunk[0] * QUAD : (quad + 1) * QUAD, :], in_=whole[:])
            elif unit < UNITS - 1:
                nc.sync.dma_start(out=out[:, n0 : n0 + QUAD, cols], in_=o[:, :, cols])

        wraw = const.tile([P, HEADS, PACK, DH], BF16)
        bias_rows = const.tile([P, P], BF16)
        nc.vector.memset(bias_rows[:], 0.0)

        load_plan = sorted(
            [(2 * c[0] - X_LEAD, 0, c) for c in X_CHUNKS] + [(2 * c[0] - SV_LEAD, 1, c) for c in SV_CHUNKS]
        )

        def trigger_loads(step):
            for due, is_sv, chunk in load_plan:
                if due == step or (step == 0 and due < 0):
                    if is_sv:
                        load_sv(chunk)
                    else:
                        load_x(chunk)

        trigger_loads(0)

        wg = const.tile([P, HEADS, DH, PACK], BF16, align_bytes=64)
        w_codes = const.tile([P, HEADS * DH], U32, align_bytes=64)
        w_scales = const.tile([P, HEADS * DH], U8, align_bytes=64)
        for h in range(HEADS):
            nc.vector.tensor_copy(out=wg[:, h], in_=wraw[:, h].rearrange("q t c -> q c t"))
            nc.vector.quantize_mx(
                out=w_codes[:, h * DH : (h + 1) * DH].bitcast(FP8X4),
                scales=w_scales[:, h * DH : (h + 1) * DH],
                in_=wg[:, h].rearrange("q c t -> q (c t)"),
            )
        bias_rows_f32 = const.tile([P, P], F32)
        bias_col = const.tile([P, D // P], F32)

        def bias_to_partitions():
            nc.vector.tensor_copy(out=bias_rows_f32[:], in_=bias_rows[:])
            bt = psum_b.tile([P, P], F32, name="bt", tag="tb")
            nc.tensor.transpose(bt[:], bias_rows_f32[:], ident[:])
            nc.vector.tensor_copy(out=bias_col[:], in_=bt[:, 0 : D // P])

        for step in range(UNITS + FINISH_LAG):
            if step > 0:
                trigger_loads(step)
            if step < UNITS:
                transpose_in(step)
            if step == MULTIPLY_LAG:
                bias_to_partitions()
            if 0 <= step - MULTIPLY_LAG < UNITS:
                quantise(step - MULTIPLY_LAG)
                multiply(step - MULTIPLY_LAG)
            if 0 <= step - BACK_LAG < UNITS:
                transpose_back(step - BACK_LAG)
            if 0 <= step - FINISH_LAG < UNITS:
                finish(step - FINISH_LAG)
